import numpy as np
import ml_dtypes


def mxq(x, axis, fmt="e4m3"):
    dtype, down = {"e4m3": (ml_dtypes.float8_e4m3fn, 7), "e5m2": (ml_dtypes.float8_e5m2, 14)}[fmt]
    v = np.moveaxis(np.asarray(x, np.float32).astype(ml_dtypes.bfloat16).astype(np.float64), axis, -1)
    blocks = v.reshape(v.shape[:-1] + (-1, 32))
    amax = np.abs(blocks).max(-1, keepdims=True)
    byte = np.maximum(np.where(amax > 0, np.frexp(amax)[1] - 1 + 127, 0) - down, 1)
    scale = np.exp2(byte - 127.0)
    codes = (blocks / scale).astype(np.float32).astype(dtype).astype(np.float64)
    return np.moveaxis((codes * scale).reshape(v.shape), -1, axis)


WIDE = False


def mx_kscale(k):
    if not WIDE:
        return np.ones(k)
    levels = np.array([10, -10, 5, -5, 0])
    a = np.random.permutation(np.resize(levels, k // 512 * 4)).reshape(k // 512, 4)
    idx = np.arange(k)
    return np.exp2(a[idx // 512, idx % 128 // 32])


BF16 = ml_dtypes.bfloat16


def bf(x):
    return np.asarray(x, np.float32).astype(BF16)


def f64(x):
    return np.asarray(x).astype(np.float64)


B, S, C, HD = 1, 512, 3072, 128
H = C // HD
HP = HD // 2
EPS = 1e-6
THETA = 10000.0


def rmsnorm(h, g):
    return h * (1.0 / np.sqrt(np.mean(h * h, axis=-1, keepdims=True) + EPS)) * g


def apply_rope1(h, freqs):
    sh = h.shape
    h_ = h.reshape(*sh[:-1], -1, 1, 2)
    out = freqs[..., 0] * h_[..., 0] + freqs[..., 1] * h_[..., 1]
    return out.reshape(sh)


def setup_inputs():
    s = mx_kscale(C)
    pos = f64(np.random.randint(0, S, size=(S, 1)))
    inv_freq = 1.0 / THETA ** (np.arange(HP) / HP)
    ang = pos * inv_freq
    cos, sin = np.cos(ang), np.sin(ang)
    rot = np.stack([np.stack([cos, -sin], -1), np.stack([sin, cos], -1)], -2)
    return {"x": bf(np.random.standard_normal((B, S, C)) * s),
            "freqs": bf(rot[None, :, None]),
            "w": bf(np.random.standard_normal((C, C)) / np.sqrt(C) / s[None, :]),
            "b": bf(np.random.standard_normal(C) * 0.3),
            "g": bf(1.0 + 0.1 * np.random.standard_normal(HD))}


def reference(x, freqs, w, b, g):
    p = (mxq(f64(x), 2, "e4m3") @ mxq(f64(w), 1, "e4m3").T) + f64(b)
    h = p.reshape(B, S, H, HD)
    return apply_rope1(rmsnorm(h, f64(g)), f64(freqs))

@@ -1,0 +1,233 @@
+from contextlib import ExitStack
+
+import concourse.mybir as mybir
+from concourse.masks import make_identity
+
+F32 = mybir.dt.float32
+BF16 = mybir.dt.bfloat16
+U32 = mybir.dt.uint32
+U8 = mybir.dt.uint8
+FP8X4 = mybir.dt.float8_e4m3fn_x4
+ACT = mybir.ActivationFunctionType
+ALU = mybir.AluOpType
+
+P = 128
+TOKENS = 512
+CHANNELS = 3072
+HEAD = 128
+PAIRS = HEAD // 2
+EPS = 1e-6
+
+K_PASS = 4 * P
+PASSES = CHANNELS // K_PASS
+WORDS = K_PASS // 2
+BLOCK = 2 * P
+X_BLOCKS = TOKENS // BLOCK
+W_BLOCKS = CHANNELS // BLOCK
+HEADS_IN_BLOCK = BLOCK // HEAD
+RAW_BUFS = 6
+
+FLOPS = 2 * TOKENS * CHANNELS * CHANNELS
+
+
+def tile_selfattention_pa_kernel(tc, x, freqs, w, b, g, out):
+    nc = tc.nc
+    x_rows = x.rearrange("o s k -> (o s) k")
+    freqs_view = freqs.rearrange("o (m p) q j i c -> p (o m q) (j i c)", p=P)
+    out_view = out.rearrange("o (m p) h d -> p (o m) (h d)", p=P)
+
+    sources = [x_rows[i * BLOCK : (i + 1) * BLOCK, :] for i in range(X_BLOCKS)]
+    sources += [w[i * BLOCK : (i + 1) * BLOCK, :] for i in range(W_BLOCKS)]
+
+    with ExitStack() as ctx:
+        ctx.enter_context(tc.manual_schedule())
+        consts = ctx.enter_context(tc.tile_pool(name="consts", bufs=1))
+        raw_pool = ctx.enter_context(tc.tile_pool(name="raw", bufs=RAW_BUFS))
+        grouped_pool = ctx.enter_context(tc.tile_pool(name="grouped", bufs=4))
+        x_mx = ctx.enter_context(tc.tile_pool(name="x_mx", bufs=1))
+        w_mx = ctx.enter_context(tc.tile_pool(name="w_mx", bufs=3))
+        work = ctx.enter_context(tc.tile_pool(name="work", bufs=3))
+        stats = ctx.enter_context(tc.tile_pool(name="stats", bufs=4))
+        flipped_psum = ctx.enter_context(tc.psum_pool(name="flipped_psum", bufs=PASSES))
+        acc_psum = ctx.enter_context(tc.psum_pool(name="acc_psum", bufs=2))
+
+        raw_tiles = {}
+
+        def load(i):
+            if i < len(sources):
+                raw = raw_pool.tile([P, 2, CHANNELS], BF16, name="raw")
+                nc.sync.dma_start(out=raw[:], in_=sources[i].rearrange("(c p) k -> p c k", p=P))
+                raw_tiles[i] = raw
+
+        for i in range(3):
+            load(i)
+
+        eps = consts.tile([P, 1], F32, name="eps")
+        nc.vector.memset(eps[:], EPS)
+        warm = consts.tile([P, 1], F32, name="warm")
+        nc.scalar.activation(out=warm[:], in_=eps[:], func=ACT.Sqrt)
+        ident = consts.tile([P, P], F32, name="ident")
+        make_identity(nc, ident[:])
+
+        freqs_sb = consts.tile([P, TOKENS // P, 4 * PAIRS], BF16, name="freqs_sb")
+        nc.sync.dma_start(out=freqs_sb[:], in_=freqs_view)
+        gain = consts.tile([P, HEAD], BF16, name="gain")
+        nc.sync.dma_start(out=gain[:], in_=g.partition_broadcast(P))
+        bias = consts.tile([P, CHANNELS], BF16, name="bias")
+        nc.sync.dma_start(out=bias[:], in_=b.partition_broadcast(P))
+        for i in range(3, RAW_BUFS):
+            load(i)
+
+        table = []
+        for c in range(2):
+            tab = consts.tile([P, TOKENS // P, PAIRS, 2], F32, name="table%d" % c)
+            nc.vector.tensor_tensor(
+                out=tab[:],
+                in0=freqs_sb[:].rearrange("p m (j i c) -> p c m j i", i=2, c=2)[:, c],
+                in1=gain[:]
+                .rearrange("p (j c) -> p c j", c=2)[:, c]
+                .unsqueeze(1)
+                .unsqueeze(3)
+                .to_broadcast([P, TOKENS // P, PAIRS, 2]),
+                op=ALU.mult,
+            )
+            table.append(tab)
+
+        def transpose_block(i):
+            words = raw_tiles.pop(i)[:].bitcast(F32)
+            banks = []
+            for q in range(PASSES):
+                flipped = flipped_psum.tile([P, 2, BLOCK], F32, name="flipped")
+                for c in range(2):
+                    for u in range(2):
+                        first = q * WORDS + u * P
+                        nc.tensor.transpose(
+                            flipped[:, u, c * P : (c + 1) * P], words[:, c, first : first + P], ident[:]
+                        )
+                banks.append(flipped)
+            load(i + RAW_BUFS)
+            return banks
+
+        def regroup(engine_copy, flipped):
+            grouped = grouped_pool.tile([P, 4 * BLOCK], BF16, name="grouped", align_bytes=64)
+            engine_copy(
+                out=grouped[:].bitcast(F32).rearrange("p (r u) -> p r u", u=2),
+                in_=flipped[:].rearrange("p u r -> p r u"),
+            )
+            return grouped
+
+        def quantise(grouped, codes, scales, q):
+            nc.vector.quantize_mx(
+                out=codes[:, q, :].bitcast(FP8X4), scales=scales[:, q, :], in_=grouped[:]
+            )
+
+        def mx_tiles(pool, name):
+            codes = pool.tile([P, PASSES, BLOCK], U32, name=name + "_codes", align_bytes=64)
+            scales = pool.tile([P, PASSES, BLOCK], U8, name=name + "_scales", align_bytes=64)
+            return codes, scales
+
+        def multiply(x_pair, w_pair):
+            acc = acc_psum.tile([P, 2, BLOCK], F32, name="acc")
+            for c in range(2):
+                for q in range(PASSES):
+                    nc.tensor.matmul_mx(
+                        out=acc[:, c, :],
+                        lhsT=x_pair[0][:, q, c * P : (c + 1) * P].bitcast(FP8X4),
+                        lhsT_scale=x_pair[1][:, q, c * P : (c + 1) * P],
+                        rhs=w_pair[0][:, q, :].bitcast(FP8X4),
+                        rhs_scale=w_pair[1][:, q, :],
+                        start=(q == 0),
+                        stop=(q == PASSES - 1),
+                    )
+            return acc
+
+        def add_bias(acc, wb):
+            u = work.tile([P, 2, BLOCK], F32, name="u")
+            nc.vector.tensor_tensor(
+                out=u[:],
+                in0=acc[:],
+                in1=bias[:, wb * BLOCK : (wb + 1) * BLOCK].unsqueeze(1).to_broadcast([P, 2, BLOCK]),
+                op=ALU.add,
+            )
+            return u
+
+        def root_mean_square(u):
+            by_head = u[:].rearrange("p c (h d) -> p (c h) d", d=HEAD)
+            squares = work.tile([P, 2 * HEADS_IN_BLOCK, HEAD], F32, name="squares")
+            sums = stats.tile([P, 2 * HEADS_IN_BLOCK], F32, name="sums")
+            for n in range(2 * HEADS_IN_BLOCK):
+                nc.scalar.activation(
+                    out=squares[:, n, :], in_=by_head[:, n, :], func=ACT.Square,
+                    accum_out=sums[:, n : n + 1],
+                )
+            rms = stats.tile([P, 2 * HEADS_IN_BLOCK], F32, name="rms")
+            nc.scalar.activation(out=rms[:], in_=sums[:], func=ACT.Sqrt, scale=1.0 / HEAD, bias=eps[:])
+            return rms
+
+        def rotate(u, xb):
+            shape = [P, 2, HEADS_IN_BLOCK, PAIRS, 2]
+            pairs = u[:].rearrange("p c (h j i) -> p c h j i", h=HEADS_IN_BLOCK, i=2)
+            products = []
+            for c in range(2):
+                product = work.tile(shape, F32, name="product%d" % c)
+                nc.vector.tensor_tensor(
+                    out=product[:],
+                    in0=pairs[:, :, :, :, c : c + 1].to_broadcast(shape),
+                    in1=table[c][:, 2 * xb : 2 * xb + 2].unsqueeze(2).to_broadcast(shape),
+                    op=ALU.mult,
+                )
+                products.append(product)
+            rotated = work.tile(shape, F32, name="rotated")
+            nc.vector.tensor_tensor(out=rotated[:], in0=products[0][:], in1=products[1][:], op=ALU.add)
+            return rotated
+
+        def invert(rms):
+            inv_rms = stats.tile([P, 2 * HEADS_IN_BLOCK], F32, name="inv_rms")
+            nc.vector.reciprocal(out=inv_rms[:], in_=rms[:])
+            return inv_rms
+
+        def scale_and_store(rotated, inv_rms, xb, wb):
+            by_head = rotated[:].rearrange("p c h j i -> p (c h) (j i)")
+            result = work.tile([P, 2 * HEADS_IN_BLOCK, HEAD], F32, name="result")
+            for n in range(2 * HEADS_IN_BLOCK):
+                nc.scalar.activation(
+                    out=result[:, n, :], in_=by_head[:, n, :], func=ACT.Copy, scale=inv_rms[:, n : n + 1]
+                )
+            nc.sync.dma_start(
+                out=out_view[:, 2 * xb : 2 * xb + 2, wb * BLOCK : (wb + 1) * BLOCK],
+                in_=result[:].rearrange("p (c h) d -> p c (h d)", c=2),
+            )
+
+        ready = []
+        for i in range(X_BLOCKS + 1):
+            pair = mx_tiles(x_mx, "x%d" % i) if i < X_BLOCKS else mx_tiles(w_mx, "w")
+            banks = transpose_block(i)
+            for q in range(PASSES):
+                grouped = regroup(nc.scalar.copy if q % 2 == 0 else nc.vector.tensor_copy, banks[q])
+                quantise(grouped, pair[0], pair[1], q)
+            ready.append(pair)
+        x_pairs = ready[:X_BLOCKS]
+        w_now = ready[X_BLOCKS]
+
+        waiting = []
+        for wb in range(W_BLOCKS + 1):
+            prepare_next = wb + 1 < W_BLOCKS
+            if prepare_next:
+                banks = transpose_block(X_BLOCKS + wb + 1)
+                w_next = mx_tiles(w_mx, "w")
+            accs = [multiply(x_pairs[xb], w_now) for xb in range(X_BLOCKS)] if wb < W_BLOCKS else []
+            for xb in range(X_BLOCKS):
+                if waiting:
+                    rms = root_mean_square(waiting[xb])
+                    rotated = rotate(waiting[xb], xb)
+                    inv_rms = invert(rms)
+                if prepare_next:
+                    half = range(xb * PASSES // 2, (xb + 1) * PASSES // 2)
+                    grouped_tiles = [regroup(nc.scalar.copy, banks[q]) for q in half]
+                    for q, grouped in zip(half, grouped_tiles):
+                        quantise(grouped, w_next[0], w_next[1], q)
+                if waiting:
+                    scale_and_store(rotated, inv_rms, xb, wb - 1)
+            waiting = [add_bias(acc, wb) for acc in accs]
+            if prepare_next:
+                w_now = w_next

@@ -26,6 +26,19 @@ X_BLOCKS = TOKENS // BLOCK
 W_BLOCKS = CHANNELS // BLOCK
 HEADS_IN_BLOCK = BLOCK // HEAD
 RAW_BUFS = 6
+HALF = PASSES // 2
+PREPARATIONS = 2 * (X_BLOCKS + W_BLOCKS)
+BANKS = X_BLOCKS * W_BLOCKS
+GROUPS = 2 * HEADS_IN_BLOCK
+
+REGROUP_LAG = 1
+QUANTISE_LAG = 2
+MULTIPLY_LAG = 2 * (X_BLOCKS + 1) + QUANTISE_LAG
+BIAS_LAG = MULTIPLY_LAG + 1
+PRODUCT_LAG = MULTIPLY_LAG + 2
+ADD_LAG = MULTIPLY_LAG + 3
+STORE_LAG = MULTIPLY_LAG + 4
+STEPS = BANKS + STORE_LAG
 
 FLOPS = 2 * TOKENS * CHANNELS * CHANNELS
 
@@ -43,24 +56,34 @@ def tile_selfattention_pa_kernel(tc, x, freqs, w, b, g, out):
         ctx.enter_context(tc.manual_schedule())
         consts = ctx.enter_context(tc.tile_pool(name="consts", bufs=1))
         raw_pool = ctx.enter_context(tc.tile_pool(name="raw", bufs=RAW_BUFS))
-        grouped_pool = ctx.enter_context(tc.tile_pool(name="grouped", bufs=4))
+        grouped_pool = ctx.enter_context(tc.tile_pool(name="grouped", bufs=3 * HALF))
         x_mx = ctx.enter_context(tc.tile_pool(name="x_mx", bufs=1))
         w_mx = ctx.enter_context(tc.tile_pool(name="w_mx", bufs=3))
         work = ctx.enter_context(tc.tile_pool(name="work", bufs=3))
         stats = ctx.enter_context(tc.tile_pool(name="stats", bufs=4))
-        flipped_psum = ctx.enter_context(tc.psum_pool(name="flipped_psum", bufs=PASSES))
+        flipped_psum = ctx.enter_context(tc.psum_pool(name="flipped_psum", bufs=2 * HALF))
         acc_psum = ctx.enter_context(tc.psum_pool(name="acc_psum", bufs=2))
 
         raw_tiles = {}
+        flipped_banks = {}
+        grouped_tiles = {}
+        mx_operands = {}
+        acc_banks = {}
+        biased = {}
+        square_sums = {}
+        rms_values = {}
+        inverse_rms = {}
+        product_tiles = {}
+        rotated_tiles = {}
 
-        def load(i):
-            if i < len(sources):
+        def load(block):
+            if block < len(sources):
                 raw = raw_pool.tile([P, 2, CHANNELS], BF16, name="raw")
-                nc.sync.dma_start(out=raw[:], in_=sources[i].rearrange("(c p) k -> p c k", p=P))
-                raw_tiles[i] = raw
+                nc.sync.dma_start(out=raw[:], in_=sources[block].rearrange("(c p) k -> p c k", p=P))
+                raw_tiles[block] = raw
 
-        for i in range(3):
-            load(i)
+        for block in range(X_BLOCKS + 1):
+            load(block)
 
         eps = consts.tile([P, 1], F32, name="eps")
         nc.vector.memset(eps[:], EPS)
@@ -75,28 +98,36 @@ def tile_selfattention_pa_kernel(tc, x, freqs, w, b, g, out):
         nc.sync.dma_start(out=gain[:], in_=g.partition_broadcast(P))
         bias = consts.tile([P, CHANNELS], BF16, name="bias")
         nc.sync.dma_start(out=bias[:], in_=b.partition_broadcast(P))
-        for i in range(3, RAW_BUFS):
-            load(i)
+        for block in range(X_BLOCKS + 1, RAW_BUFS):
+            load(block)
 
         table = []
-        for c in range(2):
-            tab = consts.tile([P, TOKENS // P, PAIRS, 2], F32, name="table%d" % c)
-            nc.vector.tensor_tensor(
-                out=tab[:],
-                in0=freqs_sb[:].rearrange("p m (j i c) -> p c m j i", i=2, c=2)[:, c],
-                in1=gain[:]
-                .rearrange("p (j c) -> p c j", c=2)[:, c]
-                .unsqueeze(1)
-                .unsqueeze(3)
-                .to_broadcast([P, TOKENS // P, PAIRS, 2]),
-                op=ALU.mult,
-            )
-            table.append(tab)
 
-        def transpose_block(i):
-            words = raw_tiles.pop(i)[:].bitcast(F32)
-            banks = []
-            for q in range(PASSES):
+        def build_tables():
+            for c in range(2):
+                tab = consts.tile([P, TOKENS // P, PAIRS, 2], F32, name="table%d" % c)
+                nc.vector.tensor_tensor(
+                    out=tab[:],
+                    in0=freqs_sb[:].rearrange("p m (j i c) -> p c m j i", i=2, c=2)[:, c],
+                    in1=gain[:]
+                    .rearrange("p (j c) -> p c j", c=2)[:, c]
+                    .unsqueeze(1)
+                    .unsqueeze(3)
+                    .to_broadcast([P, TOKENS // P, PAIRS, 2]),
+                    op=ALU.mult,
+                )
+                table.append(tab)
+
+        def passes_of(n):
+            return range((n % 2) * HALF, (n % 2 + 1) * HALF)
+
+        def transpose(n):
+            if not 0 <= n < PREPARATIONS:
+                return
+            block = n // 2
+            words = raw_tiles[block][:].bitcast(F32)
+            flipped_banks[n] = []
+            for q in passes_of(n):
                 flipped = flipped_psum.tile([P, 2, BLOCK], F32, name="flipped")
                 for c in range(2):
                     for u in range(2):
@@ -104,70 +135,99 @@ def tile_selfattention_pa_kernel(tc, x, freqs, w, b, g, out):
                         nc.tensor.transpose(
                             flipped[:, u, c * P : (c + 1) * P], words[:, c, first : first + P], ident[:]
                         )
-                banks.append(flipped)
-            load(i + RAW_BUFS)
-            return banks
+                flipped_banks[n].append(flipped)
+            if n % 2 == 1:
+                load(block + RAW_BUFS)
 
-        def regroup(engine_copy, flipped):
-            grouped = grouped_pool.tile([P, 4 * BLOCK], BF16, name="grouped", align_bytes=64)
-            engine_copy(
-                out=grouped[:].bitcast(F32).rearrange("p (r u) -> p r u", u=2),
-                in_=flipped[:].rearrange("p u r -> p r u"),
-            )
-            return grouped
+        def regroup(n):
+            if not 0 <= n < PREPARATIONS:
+                return
+            grouped_tiles[n] = []
+            for q, flipped in zip(passes_of(n), flipped_banks.pop(n)):
+                grouped = grouped_pool.tile([P, 4 * BLOCK], BF16, name="grouped", align_bytes=64)
+                copy = nc.vector.tensor_copy if q == PASSES - 1 else nc.scalar.copy
+                copy(
+                    out=grouped[:].bitcast(F32).rearrange("p (r u) -> p r u", u=2),
+                    in_=flipped[:].rearrange("p u r -> p r u"),
+                )
+                grouped_tiles[n].append(grouped)
 
-        def quantise(grouped, codes, scales, q):
-            nc.vector.quantize_mx(
-                out=codes[:, q, :].bitcast(FP8X4), scales=scales[:, q, :], in_=grouped[:]
-            )
+        def quantise(n):
+            if not 0 <= n < PREPARATIONS:
+                return
+            block = n // 2
+            if n % 2 == 0:
+                pool, name = (x_mx, "x%d" % block) if block < X_BLOCKS else (w_mx, "w")
+                codes = pool.tile([P, PASSES, BLOCK], U32, name=name + "_codes", align_bytes=64)
+                scales = pool.tile([P, PASSES, BLOCK], U8, name=name + "_scales", align_bytes=64)
+                mx_operands[block] = (codes, scales)
+            codes, scales = mx_operands[block]
+            for q, grouped in zip(passes_of(n), grouped_tiles.pop(n)):
+                nc.vector.quantize_mx(
+                    out=codes[:, q, :].bitcast(FP8X4), scales=scales[:, q, :], in_=grouped[:]
+                )
 
-        def mx_tiles(pool, name):
-            codes = pool.tile([P, PASSES, BLOCK], U32, name=name + "_codes", align_bytes=64)
-            scales = pool.tile([P, PASSES, BLOCK], U8, name=name + "_scales", align_bytes=64)
-            return codes, scales
-
-        def multiply(x_pair, w_pair):
+        def multiply(n):
+            if not 0 <= n < BANKS:
+                return
+            x_codes, x_scales = mx_operands[n % X_BLOCKS]
+            w_codes, w_scales = mx_operands[X_BLOCKS + n // X_BLOCKS]
             acc = acc_psum.tile([P, 2, BLOCK], F32, name="acc")
             for c in range(2):
                 for q in range(PASSES):
                     nc.tensor.matmul_mx(
                         out=acc[:, c, :],
-                        lhsT=x_pair[0][:, q, c * P : (c + 1) * P].bitcast(FP8X4),
-                        lhsT_scale=x_pair[1][:, q, c * P : (c + 1) * P],
-                        rhs=w_pair[0][:, q, :].bitcast(FP8X4),
-                        rhs_scale=w_pair[1][:, q, :],
+                        lhsT=x_codes[:, q, c * P : (c + 1) * P].bitcast(FP8X4),
+                        lhsT_scale=x_scales[:, q, c * P : (c + 1) * P],
+                        rhs=w_codes[:, q, :].bitcast(FP8X4),
+                        rhs_scale=w_scales[:, q, :],
                         start=(q == 0),
                         stop=(q == PASSES - 1),
                     )
-            return acc
+            acc_banks[n] = acc
 
-        def add_bias(acc, wb):
+        def add_bias(n):
+            if not 0 <= n < BANKS:
+                return
+            wb = n // X_BLOCKS
             u = work.tile([P, 2, BLOCK], F32, name="u")
             nc.vector.tensor_tensor(
                 out=u[:],
-                in0=acc[:],
+                in0=acc_banks.pop(n)[:],
                 in1=bias[:, wb * BLOCK : (wb + 1) * BLOCK].unsqueeze(1).to_broadcast([P, 2, BLOCK]),
                 op=ALU.add,
             )
-            return u
+            biased[n] = u
 
-        def root_mean_square(u):
-            by_head = u[:].rearrange("p c (h d) -> p (c h) d", d=HEAD)
-            squares = work.tile([P, 2 * HEADS_IN_BLOCK, HEAD], F32, name="squares")
-            sums = stats.tile([P, 2 * HEADS_IN_BLOCK], F32, name="sums")
-            for n in range(2 * HEADS_IN_BLOCK):
+        def sum_squares(n):
+            if not 0 <= n < BANKS:
+                return
+            by_group = biased.pop(n)[:].rearrange("p c (h d) -> p (c h) d", d=HEAD)
+            squares = work.tile([P, GROUPS, HEAD], F32, name="squares")
+            sums = stats.tile([P, GROUPS], F32, name="sums")
+            for k in range(GROUPS):
                 nc.scalar.activation(
-                    out=squares[:, n, :], in_=by_head[:, n, :], func=ACT.Square,
-                    accum_out=sums[:, n : n + 1],
+                    out=squares[:, k, :], in_=by_group[:, k, :], func=ACT.Square,
+                    accum_out=sums[:, k : k + 1],
                 )
-            rms = stats.tile([P, 2 * HEADS_IN_BLOCK], F32, name="rms")
-            nc.scalar.activation(out=rms[:], in_=sums[:], func=ACT.Sqrt, scale=1.0 / HEAD, bias=eps[:])
-            return rms
+            square_sums[n] = sums
 
-        def rotate(u, xb):
+        def root(n):
+            if not 0 <= n < BANKS:
+                return
+            rms = stats.tile([P, GROUPS], F32, name="rms")
+            nc.scalar.activation(
+                out=rms[:], in_=square_sums.pop(n)[:], func=ACT.Sqrt, scale=1.0 / HEAD, bias=eps[:]
+            )
+            rms_values[n] = rms
+
+        def multiply_by_tables(n):
+            if not 0 <= n < BANKS:
+                return
+            xb = n % X_BLOCKS
             shape = [P, 2, HEADS_IN_BLOCK, PAIRS, 2]
-            pairs = u[:].rearrange("p c (h j i) -> p c h j i", h=HEADS_IN_BLOCK, i=2)
-            products = []
+            pairs = biased[n][:].rearrange("p c (h j i) -> p c h j i", h=HEADS_IN_BLOCK, i=2)
+            product_tiles[n] = []
             for c in range(2):
                 product = work.tile(shape, F32, name="product%d" % c)
                 nc.vector.tensor_tensor(
@@ -176,58 +236,58 @@ def tile_selfattention_pa_kernel(tc, x, freqs, w, b, g, out):
                     in1=table[c][:, 2 * xb : 2 * xb + 2].unsqueeze(2).to_broadcast(shape),
                     op=ALU.mult,
                 )
-                products.append(product)
-            rotated = work.tile(shape, F32, name="rotated")
-            nc.vector.tensor_tensor(out=rotated[:], in0=products[0][:], in1=products[1][:], op=ALU.add)
-            return rotated
+                product_tiles[n].append(product)
 
-        def invert(rms):
-            inv_rms = stats.tile([P, 2 * HEADS_IN_BLOCK], F32, name="inv_rms")
-            nc.vector.reciprocal(out=inv_rms[:], in_=rms[:])
-            return inv_rms
+        def add_products(n):
+            if not 0 <= n < BANKS:
+                return
+            first, second = product_tiles.pop(n)
+            rotated = work.tile([P, GROUPS, HEAD], F32, name="rotated")
+            nc.gpsimd.tensor_tensor(
+                out=rotated[:].rearrange("p k d -> p (k d)"),
+                in0=first[:].rearrange("p c h j i -> p (c h j i)"),
+                in1=second[:].rearrange("p c h j i -> p (c h j i)"),
+                op=ALU.add,
+            )
+            rotated_tiles[n] = rotated
 
-        def scale_and_store(rotated, inv_rms, xb, wb):
-            by_head = rotated[:].rearrange("p c h j i -> p (c h) (j i)")
-            result = work.tile([P, 2 * HEADS_IN_BLOCK, HEAD], F32, name="result")
-            for n in range(2 * HEADS_IN_BLOCK):
+        def invert(n):
+            if not 0 <= n < BANKS:
+                return
+            inv_rms = stats.tile([P, GROUPS], F32, name="inv_rms")
+            nc.vector.reciprocal(out=inv_rms[:], in_=rms_values.pop(n)[:])
+            inverse_rms[n] = inv_rms
+
+        def scale_and_store(n):
+            if not 0 <= n < BANKS:
+                return
+            xb, wb = n % X_BLOCKS, n // X_BLOCKS
+            rotated, inv_rms = rotated_tiles.pop(n), inverse_rms.pop(n)
+            result = work.tile([P, GROUPS, HEAD], F32, name="result")
+            for k in range(GROUPS):
                 nc.scalar.activation(
-                    out=result[:, n, :], in_=by_head[:, n, :], func=ACT.Copy, scale=inv_rms[:, n : n + 1]
+                    out=result[:, k, :], in_=rotated[:, k, :], func=ACT.Copy, scale=inv_rms[:, k : k + 1]
                 )
             nc.sync.dma_start(
                 out=out_view[:, 2 * xb : 2 * xb + 2, wb * BLOCK : (wb + 1) * BLOCK],
                 in_=result[:].rearrange("p (c h) d -> p c (h d)", c=2),
             )
 
-        ready = []
-        for i in range(X_BLOCKS + 1):
-            pair = mx_tiles(x_mx, "x%d" % i) if i < X_BLOCKS else mx_tiles(w_mx, "w")
-            banks = transpose_block(i)
-            for q in range(PASSES):
-                grouped = regroup(nc.scalar.copy if q % 2 == 0 else nc.vector.tensor_copy, banks[q])
-                quantise(grouped, pair[0], pair[1], q)
-            ready.append(pair)
-        x_pairs = ready[:X_BLOCKS]
-        w_now = ready[X_BLOCKS]
+        def step(t):
+            multiply(t - MULTIPLY_LAG)
+            transpose(t)
+            quantise(t - QUANTISE_LAG)
+            add_bias(t - BIAS_LAG)
+            regroup(t - REGROUP_LAG)
+            multiply_by_tables(t - PRODUCT_LAG)
+            sum_squares(t - PRODUCT_LAG)
+            add_products(t - ADD_LAG)
+            invert(t - ADD_LAG)
+            scale_and_store(t - STORE_LAG)
+            root(t - PRODUCT_LAG)
 
-        waiting = []
-        for wb in range(W_BLOCKS + 1):
-            prepare_next = wb + 1 < W_BLOCKS
-            if prepare_next:
-                banks = transpose_block(X_BLOCKS + wb + 1)
-                w_next = mx_tiles(w_mx, "w")
-            accs = [multiply(x_pairs[xb], w_now) for xb in range(X_BLOCKS)] if wb < W_BLOCKS else []
-            for xb in range(X_BLOCKS):
-                if waiting:
-                    rms = root_mean_square(waiting[xb])
-                    rotated = rotate(waiting[xb], xb)
-                    inv_rms = invert(rms)
-                if prepare_next:
-                    half = range(xb * PASSES // 2, (xb + 1) * PASSES // 2)
-                    grouped_tiles = [regroup(nc.scalar.copy, banks[q]) for q in half]
-                    for q, grouped in zip(half, grouped_tiles):
-                        quantise(grouped, w_next[0], w_next[1], q)
-                if waiting:
-                    scale_and_store(rotated, inv_rms, xb, wb - 1)
-            waiting = [add_bias(acc, wb) for acc in accs]
-            if prepare_next:
-                w_now = w_next
+        for t in range(MULTIPLY_LAG):
+            step(t)
+        build_tables()
+        for t in range(MULTIPLY_LAG, STEPS):
+            step(t)

@@ -167,24 +167,23 @@ def tile_selfattention_pa_kernel(tc, x, freqs, w, b, g, out):
                     out=codes[:, q, :].bitcast(FP8X4), scales=scales[:, q, :], in_=grouped[:]
                 )
 
-        def multiply(n):
+        def multiply(n, c):
             if not 0 <= n < BANKS:
                 return
             x_codes, x_scales = mx_operands[n % X_BLOCKS]
             w_codes, w_scales = mx_operands[X_BLOCKS + n // X_BLOCKS]
-            acc = acc_psum.tile([P, 2, BLOCK], F32, name="acc")
-            for c in range(2):
-                for q in range(PASSES):
-                    nc.tensor.matmul_mx(
-                        out=acc[:, c, :],
-                        lhsT=x_codes[:, q, c * P : (c + 1) * P].bitcast(FP8X4),
-                        lhsT_scale=x_scales[:, q, c * P : (c + 1) * P],
-                        rhs=w_codes[:, q, :].bitcast(FP8X4),
-                        rhs_scale=w_scales[:, q, :],
-                        start=(q == 0),
-                        stop=(q == PASSES - 1),
-                    )
-            acc_banks[n] = acc
+            if c == 0:
+                acc_banks[n] = acc_psum.tile([P, 2, BLOCK], F32, name="acc")
+            for q in range(PASSES):
+                nc.tensor.matmul_mx(
+                    out=acc_banks[n][:, c, :],
+                    lhsT=x_codes[:, q, c * P : (c + 1) * P].bitcast(FP8X4),
+                    lhsT_scale=x_scales[:, q, c * P : (c + 1) * P],
+                    rhs=w_codes[:, q, :].bitcast(FP8X4),
+                    rhs_scale=w_scales[:, q, :],
+                    start=(q == 0),
+                    stop=(q == PASSES - 1),
+                )
 
         def add_bias(n):
             if not 0 <= n < BANKS:
@@ -274,8 +273,9 @@ def tile_selfattention_pa_kernel(tc, x, freqs, w, b, g, out):
             )
 
         def step(t):
-            multiply(t - MULTIPLY_LAG)
+            multiply(t - MULTIPLY_LAG, 0)
             transpose(t)
+            multiply(t - MULTIPLY_LAG, 1)
             quantise(t - QUANTISE_LAG)
             add_bias(t - BIAS_LAG)
             regroup(t - REGROUP_LAG)

@@ -25,20 +25,20 @@ BLOCK = 2 * P
 X_BLOCKS = TOKENS // BLOCK
 W_BLOCKS = CHANNELS // BLOCK
 HEADS_IN_BLOCK = BLOCK // HEAD
-RAW_BUFS = 6
 HALF = PASSES // 2
+RAW_BUFS = 12
 PREPARATIONS = 2 * (X_BLOCKS + W_BLOCKS)
 BANKS = X_BLOCKS * W_BLOCKS
 GROUPS = 2 * HEADS_IN_BLOCK
 
 REGROUP_LAG = 1
 QUANTISE_LAG = 2
-MULTIPLY_LAG = 2 * (X_BLOCKS + 1) + QUANTISE_LAG
-BIAS_LAG = MULTIPLY_LAG + 1
-PRODUCT_LAG = MULTIPLY_LAG + 2
-ADD_LAG = MULTIPLY_LAG + 3
-STORE_LAG = MULTIPLY_LAG + 4
-STEPS = BANKS + STORE_LAG
+MULTIPLY_LAG = 2 * X_BLOCKS + 2 + QUANTISE_LAG
+BIAS_LAG = 1
+PRODUCT_LAG = 2
+ADD_LAG = 3
+STORE_LAG = 4
+STEPS = BANKS + MULTIPLY_LAG + STORE_LAG
 
 FLOPS = 2 * TOKENS * CHANNELS * CHANNELS
 
@@ -49,8 +49,8 @@ def tile_selfattention_pa_kernel(tc, x, freqs, w, b, g, out):
     freqs_view = freqs.rearrange("o (m p) q j i c -> p (o m q) (j i c)", p=P)
     out_view = out.rearrange("o (m p) h d -> p (o m) (h d)", p=P)
 
-    sources = [x_rows[i * BLOCK : (i + 1) * BLOCK, :] for i in range(X_BLOCKS)]
-    sources += [w[i * BLOCK : (i + 1) * BLOCK, :] for i in range(W_BLOCKS)]
+    blocks = [("x", 0), ("w", 0), ("x", 1)] + [("w", i) for i in range(1, W_BLOCKS)]
+    bank_of_step = {n + MULTIPLY_LAG - max(0, 2 - n): n for n in range(BANKS)}
 
     with ExitStack() as ctx:
         ctx.enter_context(tc.manual_schedule())
@@ -76,14 +76,20 @@ def tile_selfattention_pa_kernel(tc, x, freqs, w, b, g, out):
         product_tiles = {}
         rotated_tiles = {}
 
-        def load(block):
-            if block < len(sources):
-                raw = raw_pool.tile([P, 2, CHANNELS], BF16, name="raw")
-                nc.sync.dma_start(out=raw[:], in_=sources[block].rearrange("(c p) k -> p c k", p=P))
-                raw_tiles[block] = raw
+        def load(n):
+            if n < PREPARATIONS:
+                kind, i = blocks[n // 2]
+                rows = (x_rows if kind == "x" else w)[i * BLOCK : (i + 1) * BLOCK, :]
+                first = (n % 2) * HALF * K_PASS
+                raw = raw_pool.tile([P, 2, HALF * K_PASS], BF16, name="raw")
+                nc.sync.dma_start(
+                    out=raw[:],
+                    in_=rows[:, first : first + HALF * K_PASS].rearrange("(c p) k -> p c k", p=P),
+                )
+                raw_tiles[n] = raw
 
-        for block in range(X_BLOCKS + 1):
-            load(block)
+        for n in range(4):
+            load(n)
 
         eps = consts.tile([P, 1], F32, name="eps")
         nc.vector.memset(eps[:], EPS)
@@ -98,8 +104,8 @@ def tile_selfattention_pa_kernel(tc, x, freqs, w, b, g, out):
         nc.sync.dma_start(out=gain[:], in_=g.partition_broadcast(P))
         bias = consts.tile([P, CHANNELS], BF16, name="bias")
         nc.sync.dma_start(out=bias[:], in_=b.partition_broadcast(P))
-        for block in range(X_BLOCKS + 1, RAW_BUFS):
-            load(block)
+        for n in range(4, RAW_BUFS):
+            load(n)
 
         table = []
 
@@ -124,29 +130,26 @@ def tile_selfattention_pa_kernel(tc, x, freqs, w, b, g, out):
         def transpose(n):
             if not 0 <= n < PREPARATIONS:
                 return
-            block = n // 2
-            words = raw_tiles[block][:].bitcast(F32)
+            words = raw_tiles.pop(n)[:].bitcast(F32)
             flipped_banks[n] = []
-            for q in passes_of(n):
+            for local in range(HALF):
                 flipped = flipped_psum.tile([P, 2, BLOCK], F32, name="flipped")
                 for c in range(2):
                     for u in range(2):
-                        first = q * WORDS + u * P
+                        first = local * WORDS + u * P
                         nc.tensor.transpose(
                             flipped[:, u, c * P : (c + 1) * P], words[:, c, first : first + P], ident[:]
                         )
                 flipped_banks[n].append(flipped)
-            if n % 2 == 1:
-                load(block + RAW_BUFS)
+            load(n + RAW_BUFS)
 
         def regroup(n):
             if not 0 <= n < PREPARATIONS:
                 return
             grouped_tiles[n] = []
-            for q, flipped in zip(passes_of(n), flipped_banks.pop(n)):
+            for flipped in flipped_banks.pop(n):
                 grouped = grouped_pool.tile([P, 4 * BLOCK], BF16, name="grouped", align_bytes=64)
-                copy = nc.vector.tensor_copy if q == PASSES - 1 else nc.scalar.copy
-                copy(
+                nc.scalar.copy(
                     out=grouped[:].bitcast(F32).rearrange("p (r u) -> p r u", u=2),
                     in_=flipped[:].rearrange("p u r -> p r u"),
                 )
@@ -155,9 +158,9 @@ def tile_selfattention_pa_kernel(tc, x, freqs, w, b, g, out):
         def quantise(n):
             if not 0 <= n < PREPARATIONS:
                 return
-            block = n // 2
+            block = blocks[n // 2]
             if n % 2 == 0:
-                pool, name = (x_mx, "x%d" % block) if block < X_BLOCKS else (w_mx, "w")
+                pool, name = (x_mx, "x%d" % block[1]) if block[0] == "x" else (w_mx, "w")
                 codes = pool.tile([P, PASSES, BLOCK], U32, name=name + "_codes", align_bytes=64)
                 scales = pool.tile([P, PASSES, BLOCK], U8, name=name + "_scales", align_bytes=64)
                 mx_operands[block] = (codes, scales)
@@ -167,26 +170,27 @@ def tile_selfattention_pa_kernel(tc, x, freqs, w, b, g, out):
                     out=codes[:, q, :].bitcast(FP8X4), scales=scales[:, q, :], in_=grouped[:]
                 )
 
-        def multiply(n, c):
-            if not 0 <= n < BANKS:
+        def multiply(n):
+            if n is None:
                 return
-            x_codes, x_scales = mx_operands[n % X_BLOCKS]
-            w_codes, w_scales = mx_operands[X_BLOCKS + n // X_BLOCKS]
-            if c == 0:
-                acc_banks[n] = acc_psum.tile([P, 2, BLOCK], F32, name="acc")
-            for q in range(PASSES):
-                nc.tensor.matmul_mx(
-                    out=acc_banks[n][:, c, :],
-                    lhsT=x_codes[:, q, c * P : (c + 1) * P].bitcast(FP8X4),
-                    lhsT_scale=x_scales[:, q, c * P : (c + 1) * P],
-                    rhs=w_codes[:, q, :].bitcast(FP8X4),
-                    rhs_scale=w_scales[:, q, :],
-                    start=(q == 0),
-                    stop=(q == PASSES - 1),
-                )
+            x_codes, x_scales = mx_operands[("x", n % X_BLOCKS)]
+            w_codes, w_scales = mx_operands[("w", n // X_BLOCKS)]
+            acc = acc_psum.tile([P, 2, BLOCK], F32, name="acc")
+            for c in range(2):
+                for q in range(PASSES):
+                    nc.tensor.matmul_mx(
+                        out=acc[:, c, :],
+                        lhsT=x_codes[:, q, c * P : (c + 1) * P].bitcast(FP8X4),
+                        lhsT_scale=x_scales[:, q, c * P : (c + 1) * P],
+                        rhs=w_codes[:, q, :].bitcast(FP8X4),
+                        rhs_scale=w_scales[:, q, :],
+                        start=(q == 0),
+                        stop=(q == PASSES - 1),
+                    )
+            acc_banks[n] = acc
 
         def add_bias(n):
-            if not 0 <= n < BANKS:
+            if n is None:
                 return
             wb = n // X_BLOCKS
             u = work.tile([P, 2, BLOCK], F32, name="u")
@@ -199,7 +203,7 @@ def tile_selfattention_pa_kernel(tc, x, freqs, w, b, g, out):
             biased[n] = u
 
         def sum_squares(n):
-            if not 0 <= n < BANKS:
+            if n is None:
                 return
             by_group = biased.pop(n)[:].rearrange("p c (h d) -> p (c h) d", d=HEAD)
             squares = work.tile([P, GROUPS, HEAD], F32, name="squares")
@@ -212,7 +216,7 @@ def tile_selfattention_pa_kernel(tc, x, freqs, w, b, g, out):
             square_sums[n] = sums
 
         def root(n):
-            if not 0 <= n < BANKS:
+            if n is None:
                 return
             rms = stats.tile([P, GROUPS], F32, name="rms")
             nc.scalar.activation(
@@ -221,7 +225,7 @@ def tile_selfattention_pa_kernel(tc, x, freqs, w, b, g, out):
             rms_values[n] = rms
 
         def multiply_by_tables(n):
-            if not 0 <= n < BANKS:
+            if n is None:
                 return
             xb = n % X_BLOCKS
             shape = [P, 2, HEADS_IN_BLOCK, PAIRS, 2]
@@ -238,11 +242,11 @@ def tile_selfattention_pa_kernel(tc, x, freqs, w, b, g, out):
                 product_tiles[n].append(product)
 
         def add_products(n):
-            if not 0 <= n < BANKS:
+            if n is None:
                 return
             first, second = product_tiles.pop(n)
             rotated = work.tile([P, GROUPS, HEAD], F32, name="rotated")
-            nc.gpsimd.tensor_tensor(
+            nc.vector.tensor_tensor(
                 out=rotated[:].rearrange("p k d -> p (k d)"),
                 in0=first[:].rearrange("p c h j i -> p (c h j i)"),
                 in1=second[:].rearrange("p c h j i -> p (c h j i)"),
@@ -251,14 +255,14 @@ def tile_selfattention_pa_kernel(tc, x, freqs, w, b, g, out):
             rotated_tiles[n] = rotated
 
         def invert(n):
-            if not 0 <= n < BANKS:
+            if n is None:
                 return
             inv_rms = stats.tile([P, GROUPS], F32, name="inv_rms")
             nc.vector.reciprocal(out=inv_rms[:], in_=rms_values.pop(n)[:])
             inverse_rms[n] = inv_rms
 
         def scale_and_store(n):
-            if not 0 <= n < BANKS:
+            if n is None:
                 return
             xb, wb = n % X_BLOCKS, n // X_BLOCKS
             rotated, inv_rms = rotated_tiles.pop(n), inverse_rms.pop(n)
@@ -273,21 +277,24 @@ def tile_selfattention_pa_kernel(tc, x, freqs, w, b, g, out):
             )
 
         def step(t):
-            multiply(t - MULTIPLY_LAG, 0)
-            transpose(t)
-            multiply(t - MULTIPLY_LAG, 1)
-            quantise(t - QUANTISE_LAG)
-            add_bias(t - BIAS_LAG)
+            add_bias(bank_of_step.get(t - BIAS_LAG))
             regroup(t - REGROUP_LAG)
-            multiply_by_tables(t - PRODUCT_LAG)
-            sum_squares(t - PRODUCT_LAG)
-            add_products(t - ADD_LAG)
-            invert(t - ADD_LAG)
-            scale_and_store(t - STORE_LAG)
-            root(t - PRODUCT_LAG)
+            if t % 2 == 0:
+                multiply(bank_of_step.get(t))
+                multiply(bank_of_step.get(t + 1))
+                transpose(t)
+                transpose(t + 1)
+            quantise(t - QUANTISE_LAG)
+            multiply_by_tables(bank_of_step.get(t - PRODUCT_LAG))
+            sum_squares(bank_of_step.get(t - PRODUCT_LAG))
+            add_products(bank_of_step.get(t - ADD_LAG))
+            invert(bank_of_step.get(t - ADD_LAG))
+            scale_and_store(bank_of_step.get(t - STORE_LAG))
+            root(bank_of_step.get(t - PRODUCT_LAG))
 
-        for t in range(MULTIPLY_LAG):
+        first_multiply = min(bank_of_step)
+        for t in range(first_multiply):
             step(t)
         build_tables()
-        for t in range(MULTIPLY_LAG, STEPS):
+        for t in range(first_multiply, STEPS):
             step(t)

from contextlib import ExitStack

import concourse.mybir as mybir
from concourse.masks import make_identity

F32 = mybir.dt.float32
BF16 = mybir.dt.bfloat16
U32 = mybir.dt.uint32
U8 = mybir.dt.uint8
FP8X4 = mybir.dt.float8_e4m3fn_x4
ACT = mybir.ActivationFunctionType
ALU = mybir.AluOpType

P = 128
TOKENS = 512
CHANNELS = 3072
HEAD = 128
PAIRS = HEAD // 2
EPS = 1e-6

K_PASS = 4 * P
PASSES = CHANNELS // K_PASS
WORDS = K_PASS // 2
BLOCK = 2 * P
X_BLOCKS = TOKENS // BLOCK
W_BLOCKS = CHANNELS // BLOCK
HEADS_IN_BLOCK = BLOCK // HEAD
HALF = PASSES // 2
RAW_BUFS = 12
PREPARATIONS = 2 * (X_BLOCKS + W_BLOCKS)
BANKS = X_BLOCKS * W_BLOCKS
GROUPS = 2 * HEADS_IN_BLOCK

REGROUP_LAG = 1
QUANTISE_LAG = 2
MULTIPLY_LAG = 2 * X_BLOCKS + 2 + QUANTISE_LAG
BIAS_LAG = 1
PRODUCT_LAG = 2
ADD_LAG = 3
STORE_LAG = 4
STEPS = BANKS + MULTIPLY_LAG + STORE_LAG

FLOPS = 2 * TOKENS * CHANNELS * CHANNELS


def tile_selfattention_pa_kernel(tc, x, freqs, w, b, g, out):
    nc = tc.nc
    x_rows = x.rearrange("o s k -> (o s) k")
    freqs_view = freqs.rearrange("o (m p) q j i c -> p (o m q) (j i c)", p=P)
    out_view = out.rearrange("o (m p) h d -> p (o m) (h d)", p=P)

    blocks = [("x", 0), ("w", 0), ("x", 1)] + [("w", i) for i in range(1, W_BLOCKS)]
    bank_of_step = {n + MULTIPLY_LAG - max(0, 2 - n): n for n in range(BANKS)}

    with ExitStack() as ctx:
        ctx.enter_context(tc.manual_schedule())
        consts = ctx.enter_context(tc.tile_pool(name="consts", bufs=1))
        raw_pool = ctx.enter_context(tc.tile_pool(name="raw", bufs=RAW_BUFS))
        grouped_pool = ctx.enter_context(tc.tile_pool(name="grouped", bufs=3 * HALF))
        x_mx = ctx.enter_context(tc.tile_pool(name="x_mx", bufs=1))
        w_mx = ctx.enter_context(tc.tile_pool(name="w_mx", bufs=3))
        work = ctx.enter_context(tc.tile_pool(name="work", bufs=3))
        stats = ctx.enter_context(tc.tile_pool(name="stats", bufs=4))
        flipped_psum = ctx.enter_context(tc.psum_pool(name="flipped_psum", bufs=2 * HALF))
        acc_psum = ctx.enter_context(tc.psum_pool(name="acc_psum", bufs=2))

        raw_tiles = {}
        flipped_banks = {}
        grouped_tiles = {}
        mx_operands = {}
        acc_banks = {}
        biased = {}
        square_sums = {}
        rms_values = {}
        inverse_rms = {}
        product_tiles = {}
        rotated_tiles = {}

        def load(n):
            if n < PREPARATIONS:
                kind, i = blocks[n // 2]
                rows = (x_rows if kind == "x" else w)[i * BLOCK : (i + 1) * BLOCK, :]
                first = (n % 2) * HALF * K_PASS
                raw = raw_pool.tile([P, 2, HALF * K_PASS], BF16, name="raw")
                nc.sync.dma_start(
                    out=raw[:],
                    in_=rows[:, first : first + HALF * K_PASS].rearrange("(c p) k -> p c k", p=P),
                )
                raw_tiles[n] = raw

        for n in range(4):
            load(n)

        eps = consts.tile([P, 1], F32, name="eps")
        nc.vector.memset(eps[:], EPS)
        warm = consts.tile([P, 1], F32, name="warm")
        nc.scalar.activation(out=warm[:], in_=eps[:], func=ACT.Sqrt)
        ident = consts.tile([P, P], F32, name="ident")
        make_identity(nc, ident[:])

        freqs_sb = consts.tile([P, TOKENS // P, 4 * PAIRS], BF16, name="freqs_sb")
        nc.sync.dma_start(out=freqs_sb[:], in_=freqs_view)
        gain = consts.tile([P, HEAD], BF16, name="gain")
        nc.sync.dma_start(out=gain[:], in_=g.partition_broadcast(P))
        bias = consts.tile([P, CHANNELS], BF16, name="bias")
        nc.sync.dma_start(out=bias[:], in_=b.partition_broadcast(P))
        for n in range(4, RAW_BUFS):
            load(n)

        table = []

        def build_tables():
            for c in range(2):
                tab = consts.tile([P, TOKENS // P, PAIRS, 2], F32, name="table%d" % c)
                nc.vector.tensor_tensor(
                    out=tab[:],
                    in0=freqs_sb[:].rearrange("p m (j i c) -> p c m j i", i=2, c=2)[:, c],
                    in1=gain[:]
                    .rearrange("p (j c) -> p c j", c=2)[:, c]
                    .unsqueeze(1)
                    .unsqueeze(3)
                    .to_broadcast([P, TOKENS // P, PAIRS, 2]),
                    op=ALU.mult,
                )
                table.append(tab)

        def passes_of(n):
            return range((n % 2) * HALF, (n % 2 + 1) * HALF)

        def transpose(n):
            if not 0 <= n < PREPARATIONS:
                return
            words = raw_tiles.pop(n)[:].bitcast(F32)
            flipped_banks[n] = []
            for local in range(HALF):
                flipped = flipped_psum.tile([P, 2, BLOCK], F32, name="flipped")
                for c in range(2):
                    for u in range(2):
                        first = local * WORDS + u * P
                        nc.tensor.transpose(
                            flipped[:, u, c * P : (c + 1) * P], words[:, c, first : first + P], ident[:]
                        )
                flipped_banks[n].append(flipped)
            load(n + RAW_BUFS)

        def regroup(n):
            if not 0 <= n < PREPARATIONS:
                return
            grouped_tiles[n] = []
            for flipped in flipped_banks.pop(n):
                grouped = grouped_pool.tile([P, 4 * BLOCK], BF16, name="grouped", align_bytes=64)
                nc.scalar.copy(
                    out=grouped[:].bitcast(F32).rearrange("p (r u) -> p r u", u=2),
                    in_=flipped[:].rearrange("p u r -> p r u"),
                )
                grouped_tiles[n].append(grouped)

        def quantise(n):
            if not 0 <= n < PREPARATIONS:
                return
            block = blocks[n // 2]
            if n % 2 == 0:
                pool, name = (x_mx, "x%d" % block[1]) if block[0] == "x" else (w_mx, "w")
                codes = pool.tile([P, PASSES, BLOCK], U32, name=name + "_codes", align_bytes=64)
                scales = pool.tile([P, PASSES, BLOCK], U8, name=name + "_scales", align_bytes=64)
                mx_operands[block] = (codes, scales)
            codes, scales = mx_operands[block]
            for q, grouped in zip(passes_of(n), grouped_tiles.pop(n)):
                nc.vector.quantize_mx(
                    out=codes[:, q, :].bitcast(FP8X4), scales=scales[:, q, :], in_=grouped[:]
                )

        def multiply(n):
            if n is None:
                return
            x_codes, x_scales = mx_operands[("x", n % X_BLOCKS)]
            w_codes, w_scales = mx_operands[("w", n // X_BLOCKS)]
            acc = acc_psum.tile([P, 2, BLOCK], F32, name="acc")
            for c in range(2):
                for q in range(PASSES):
                    nc.tensor.matmul_mx(
                        out=acc[:, c, :],
                        lhsT=x_codes[:, q, c * P : (c + 1) * P].bitcast(FP8X4),
                        lhsT_scale=x_scales[:, q, c * P : (c + 1) * P],
                        rhs=w_codes[:, q, :].bitcast(FP8X4),
                        rhs_scale=w_scales[:, q, :],
                        start=(q == 0),
                        stop=(q == PASSES - 1),
                    )
            acc_banks[n] = acc

        def add_bias(n):
            if n is None:
                return
            wb = n // X_BLOCKS
            u = work.tile([P, 2, BLOCK], F32, name="u")
            nc.vector.tensor_tensor(
                out=u[:],
                in0=acc_banks.pop(n)[:],
                in1=bias[:, wb * BLOCK : (wb + 1) * BLOCK].unsqueeze(1).to_broadcast([P, 2, BLOCK]),
                op=ALU.add,
            )
            biased[n] = u

        def sum_squares(n):
            if n is None:
                return
            by_group = biased.pop(n)[:].rearrange("p c (h d) -> p (c h) d", d=HEAD)
            squares = work.tile([P, GROUPS, HEAD], F32, name="squares")
            sums = stats.tile([P, GROUPS], F32, name="sums")
            for k in range(GROUPS):
                nc.scalar.activation(
                    out=squares[:, k, :], in_=by_group[:, k, :], func=ACT.Square,
                    accum_out=sums[:, k : k + 1],
                )
            square_sums[n] = sums

        def root(n):
            if n is None:
                return
            rms = stats.tile([P, GROUPS], F32, name="rms")
            nc.scalar.activation(
                out=rms[:], in_=square_sums.pop(n)[:], func=ACT.Sqrt, scale=1.0 / HEAD, bias=eps[:]
            )
            rms_values[n] = rms

        def multiply_by_tables(n):
            if n is None:
                return
            xb = n % X_BLOCKS
            shape = [P, 2, HEADS_IN_BLOCK, PAIRS, 2]
            pairs = biased[n][:].rearrange("p c (h j i) -> p c h j i", h=HEADS_IN_BLOCK, i=2)
            product_tiles[n] = []
            for c in range(2):
                product = work.tile(shape, F32, name="product%d" % c)
                nc.vector.tensor_tensor(
                    out=product[:],
                    in0=pairs[:, :, :, :, c : c + 1].to_broadcast(shape),
                    in1=table[c][:, 2 * xb : 2 * xb + 2].unsqueeze(2).to_broadcast(shape),
                    op=ALU.mult,
                )
                product_tiles[n].append(product)

        def add_products(n):
            if n is None:
                return
            first, second = product_tiles.pop(n)
            rotated = work.tile([P, GROUPS, HEAD], F32, name="rotated")
            nc.vector.tensor_tensor(
                out=rotated[:].rearrange("p k d -> p (k d)"),
                in0=first[:].rearrange("p c h j i -> p (c h j i)"),
                in1=second[:].rearrange("p c h j i -> p (c h j i)"),
                op=ALU.add,
            )
            rotated_tiles[n] = rotated

        def invert(n):
            if n is None:
                return
            inv_rms = stats.tile([P, GROUPS], F32, name="inv_rms")
            nc.vector.reciprocal(out=inv_rms[:], in_=rms_values.pop(n)[:])
            inverse_rms[n] = inv_rms

        def scale_and_store(n):
            if n is None:
                return
            xb, wb = n % X_BLOCKS, n // X_BLOCKS
            rotated, inv_rms = rotated_tiles.pop(n), inverse_rms.pop(n)
            result = work.tile([P, GROUPS, HEAD], F32, name="result")
            for k in range(GROUPS):
                nc.scalar.activation(
                    out=result[:, k, :], in_=rotated[:, k, :], func=ACT.Copy, scale=inv_rms[:, k : k + 1]
                )
            nc.sync.dma_start(
                out=out_view[:, 2 * xb : 2 * xb + 2, wb * BLOCK : (wb + 1) * BLOCK],
                in_=result[:].rearrange("p (c h) d -> p c (h d)", c=2),
            )

        def step(t):
            add_bias(bank_of_step.get(t - BIAS_LAG))
            regroup(t - REGROUP_LAG)
            if t % 2 == 0:
                multiply(bank_of_step.get(t))
                multiply(bank_of_step.get(t + 1))
                transpose(t)
                transpose(t + 1)
            quantise(t - QUANTISE_LAG)
            multiply_by_tables(bank_of_step.get(t - PRODUCT_LAG))
            sum_squares(bank_of_step.get(t - PRODUCT_LAG))
            add_products(bank_of_step.get(t - ADD_LAG))
            invert(bank_of_step.get(t - ADD_LAG))
            scale_and_store(bank_of_step.get(t - STORE_LAG))
            root(bank_of_step.get(t - PRODUCT_LAG))

        first_multiply = min(bank_of_step)
        for t in range(first_multiply):
            step(t)
        build_tables()
        for t in range(first_multiply, STEPS):
            step(t)
